import numpy as np
import ml_dtypes


def mxq(x, axis, fmt="e4m3"):
    dtype, down = {"e4m3": (ml_dtypes.float8_e4m3fn, 7), "e5m2": (ml_dtypes.float8_e5m2, 14)}[fmt]
    v = np.moveaxis(np.asarray(x, np.float32).astype(ml_dtypes.bfloat16).astype(np.float64), axis, -1)
    blocks = v.reshape(v.shape[:-1] + (-1, 32))
    amax = np.abs(blocks).max(-1, keepdims=True)
    byte = np.maximum(np.where(amax > 0, np.frexp(amax)[1] - 1 + 127, 0) - down, 1)
    scale = np.exp2(byte - 127.0)
    codes = (blocks / scale).astype(np.float32).astype(dtype).astype(np.float64)
    return np.moveaxis((codes * scale).reshape(v.shape), -1, axis)


WIDE = False


def mx_kscale(k):
    if not WIDE:
        return np.ones(k)
    levels = np.array([10, -10, 5, -5, 0])
    a = np.random.permutation(np.resize(levels, k // 512 * 4)).reshape(k // 512, 4)
    idx = np.arange(k)
    return np.exp2(a[idx // 512, idx % 128 // 32])


BF16 = ml_dtypes.bfloat16


def bf(x):
    return np.asarray(x, np.float32).astype(BF16)


def f64(x):
    return np.asarray(x).astype(np.float64)


N, E, H = 2048, 512, 512
LN_EPS = 1e-5
DEG_MIN = 1e-6


def erf(v):
    a = np.clip(v, -6.0, 6.0)
    term = a
    total = a
    for n in range(1, 100):
        term = term * (2.0 * a * a) / (2 * n + 1)
        total = total + term
    return 2.0 / np.sqrt(np.pi) * np.exp(-a * a) * total


def gelu(v):
    return 0.5 * v * (1.0 + erf(v / np.sqrt(2.0)))


def layer_norm(v, g, b):
    mu = v.mean(axis=-1, keepdims=True)
    var = ((v - mu) ** 2).mean(axis=-1, keepdims=True)
    return (v - mu) / np.sqrt(var + LN_EPS) * g + b


def draw_adj_norm():
    u = np.random.random((N, N))
    strong = np.random.random((N, N)) < 1.0 / np.sqrt(N)
    a = u * np.where(strong, 1.0, 1.0 / N)
    d = np.clip(a.sum(axis=1), DEG_MIN, None) ** -0.5
    return d[:, None] * a * d[None, :]


def setup_inputs():
    s, t = mx_kscale(N), mx_kscale(H)
    return {"adj_norm": bf(draw_adj_norm() * s[None, :]),
            "h1": bf(gelu(np.random.standard_normal((N, H))) / s[:, None] * t[None, :]),
            "W2": bf(np.random.standard_normal((E, H)) / np.sqrt(H) / t[None, :]),
            "b2": bf(0.1 * np.random.standard_normal(E)),
            "g2": bf(1.0 + 0.1 * np.random.standard_normal(E)),
            "beta2": bf(0.1 * np.random.standard_normal(E)),
            "residual": bf(np.random.standard_normal((N, E)))}


def reference(adj_norm, h1, W2, b2, g2, beta2, residual):
    agg = mxq(f64(adj_norm), 1, "e4m3") @ mxq(f64(h1), 0, "e4m3")
    lin = (mxq(agg, 1, "e4m3") @ mxq(f64(W2), 1, "e4m3").T) + f64(b2)
    return gelu(layer_norm(lin, f64(g2), f64(beta2))) + f64(residual)

@@ -1,0 +1,280 @@
+from contextlib import ExitStack
+
+import concourse.masks as masks
+import concourse.mybir as mybir
+
+FP8X4 = mybir.dt.float8_e4m3fn_x4
+BF16 = mybir.dt.bfloat16
+F32 = mybir.dt.float32
+U32 = mybir.dt.uint32
+U8 = mybir.dt.uint8
+ALU = mybir.AluOpType
+ACT = mybir.ActivationFunctionType
+
+P = 128
+NODES = 2048
+FEAT = 512
+TILES = NODES // P
+PASSES = NODES // 512
+LN_EPS = 1e-5
+
+FLOPS = 2 * NODES * NODES * FEAT + 2 * NODES * FEAT * FEAT
+
+LEAD = 2
+SCHED = (
+    ("GE", LEAD + 4), ("QA", LEAD + 1), ("T", 0), ("M", LEAD), ("N", LEAD + 1), ("Y", LEAD + 2),
+    ("A", LEAD + 2), ("B", LEAD + 3), ("C", 0), ("Q", 0), ("SQ", LEAD + 2), ("CA", LEAD),
+    ("D", LEAD + 4), ("R", LEAD + 2), ("ST", LEAD + 4),
+)
+LOADS = (
+    "h0", "a0", "h1", "h2", "a1", "h3", "w", "a2", "a3", "a4", "a5", "a6", "a7", "a8", "r0",
+    "a9", "a10", "a11", "a12", "r1", "a13", "a14", "a15", "r2", "r3",
+)
+
+
+def tile_multilayergnn_pb_kernel(tc, adj_norm, h1, W2, b2, g2, beta2, residual, out):
+    nc = tc.nc
+    with ExitStack() as ctx:
+        keep = ctx.enter_context(tc.tile_pool(name="keep", bufs=1))
+        rot3 = ctx.enter_context(tc.tile_pool(name="rot3", bufs=3))
+        rot4 = ctx.enter_context(tc.tile_pool(name="rot4", bufs=4))
+        rot6 = ctx.enter_context(tc.tile_pool(name="rot6", bufs=6))
+        ps_tp = ctx.enter_context(tc.psum_pool(name="ps_tp", bufs=4))
+        ps_agg = ctx.enter_context(tc.psum_pool(name="ps_agg", bufs=2))
+        ps_lin = ctx.enter_context(tc.psum_pool(name="ps_lin", bufs=2))
+        ctx.enter_context(tc.manual_schedule())
+
+        adj_raw = [keep.tile([P, NODES], BF16, name="adj_raw%d" % i) for i in range(TILES)]
+        res = [keep.tile([P, 4, FEAT], BF16, name="res%d" % c) for c in range(4)]
+        h1raw = keep.tile([P, PASSES, 4, FEAT], BF16)
+        h1g = keep.tile([P, PASSES, FEAT, 4], BF16, align_bytes=64)
+        h1c = keep.tile([P, PASSES, FEAT], U32, align_bytes=64)
+        h1s = keep.tile([P, PASSES, FEAT], U8, align_bytes=64)
+        w2raw = keep.tile([P, 4, FEAT], BF16)
+        w2g = keep.tile([P, 4, P, 4], BF16, align_bytes=64)
+        w2c = keep.tile([P, FEAT], U32, align_bytes=64)
+        w2s = keep.tile([P, FEAT], U8, align_bytes=64)
+        cst = keep.tile([P, 3, FEAT], BF16)
+        ones = keep.tile([P, P], BF16)
+        identf = keep.tile([P, P], F32)
+        identb = keep.tile([P, P], BF16)
+        neghalf = keep.tile([P, 1], F32)
+        bcast = [keep.tile([P, FEAT], F32, name="bcast%d" % j) for j in range(3)]
+
+        nc.vector.memset(cst[:], 0.0)
+        nc.vector.memset(ones[:], 1.0)
+        nc.vector.memset(neghalf[:], -0.5)
+        masks.make_identity(nc, identf[:])
+        masks.make_identity(nc, identb[:])
+
+        adj_t = adj_norm.rearrange("(a p) k -> a p k", p=P)
+        h1_t = h1.rearrange("(g u p e) h -> g p u (e h)", g=PASSES, u=2, p=P, e=2)
+        res_t = residual.rearrange("(c a p) e -> c p a e", c=4, a=4, p=P)
+        out_t = out.rearrange("(a p) e -> a p e", p=P)
+        for j, vec in enumerate((b2, g2, beta2)):
+            nc.scalar.dma_start(out=cst[0:1, j, :], in_=vec.unsqueeze(0))
+        for item in LOADS:
+            kind = item[0]
+            if kind == "a":
+                i = int(item[1:])
+                nc.sync.dma_start(out=adj_raw[i][:], in_=adj_t[i])
+            elif kind == "h":
+                g = int(item[1:])
+                nc.sync.dma_start(
+                    out=h1raw[:, g].rearrange("p (u e) h -> p u (e h)", u=2, e=2), in_=h1_t[g]
+                )
+            elif kind == "r":
+                c = int(item[1:])
+                nc.sync.dma_start(out=res[c][:], in_=res_t[c])
+            else:
+                nc.sync.dma_start(out=w2raw[:], in_=W2.rearrange("(a p) h -> p a h", p=P))
+
+        def h1_regroup(g):
+            nc.vector.tensor_copy(
+                out=h1g[:, g].rearrange("p (c i) t -> p c t i", i=4),
+                in_=h1raw[:, g].rearrange("p t (c i) -> p c t i", i=4),
+            )
+
+        def h1_quantise(g):
+            nc.vector.quantize_mx(
+                out=h1c[:, g].bitcast(FP8X4),
+                scales=h1s[:, g],
+                in_=h1g[:, g].rearrange("p h t -> p (h t)"),
+            )
+
+        h1_regroup(0)
+        for g in range(1, PASSES):
+            h1_regroup(g)
+            h1_quantise(g - 1)
+        h1_quantise(PASSES - 1)
+
+        def st_consts():
+            for j in range(3):
+                pb = ps_lin.tile([P, FEAT], F32, tag="lin")
+                nc.tensor.matmul(out=pb[:], lhsT=ones[:], rhs=cst[:, j, :], start=True, stop=True)
+                nc.scalar.copy(out=bcast[j][:], in_=pb[:])
+
+        b2bc, gbc, betabc = bcast
+
+        def st_W():
+            for half in range(2):
+                pw = ps_tp.tile([P, 2, 4, P], BF16, tag="tp")
+                for a in range(2):
+                    for t in range(4):
+                        nc.tensor.transpose(
+                            pw[:, a, t, :], w2raw[:, 2 * half + a, t * P : (t + 1) * P], identb[:]
+                        )
+                nc.scalar.copy(
+                    out=w2g[:, 2 * half : 2 * half + 2], in_=pw[:].rearrange("p a t e -> p a e t")
+                )
+            nc.vector.quantize_mx(
+                out=w2c[:].bitcast(FP8X4), scales=w2s[:], in_=w2g[:].rearrange("p a e t -> p (a e t)")
+            )
+
+        live = {}
+
+        def st_T(i):
+            words = adj_raw[i][:].bitcast(F32)
+            for b in range(2):
+                tp = ps_tp.tile([P, 2, 2, P], F32, tag="tp")
+                for gg in range(2):
+                    for u in range(2):
+                        w0 = 256 * (2 * b + gg) + P * u
+                        nc.tensor.transpose(tp[:, gg, u, :], words[:, w0 : w0 + P], identf[:])
+                live[("tp", i, b)] = tp
+
+        def st_C(i):
+            adjg = rot3.tile([P, PASSES, P, 4], BF16, align_bytes=64, tag="adjg")
+            adjgf = adjg[:].bitcast(F32)
+            for b in range(2):
+                tp = live[("tp", i, b)]
+                nc.scalar.copy(
+                    out=adjgf[:, 2 * b : 2 * b + 2], in_=tp[:].rearrange("p g u i -> p g i u")
+                )
+            live[("adjg", i)] = adjg
+
+        def st_Q(i):
+            adjg = live[("adjg", i)]
+            adjc = rot4.tile([P, PASSES * P], U32, align_bytes=64, tag="adjc")
+            adjs = rot4.tile([P, PASSES * P], U8, align_bytes=64, tag="adjs")
+            nc.vector.quantize_mx(
+                out=adjc[:].bitcast(FP8X4), scales=adjs[:], in_=adjg[:].rearrange("p g i t -> p (g i t)")
+            )
+            live[("adjq", i)] = (adjc, adjs)
+
+        def st_M(i):
+            adjc, adjs = live[("adjq", i)]
+            aggp = ps_agg.tile([P, 4, P], F32, tag="agg")
+            for t in range(4):
+                for g in range(PASSES):
+                    nc.tensor.matmul_mx(
+                        out=aggp[:, t, :],
+                        lhsT=h1c[:, g, t * P : (t + 1) * P].bitcast(FP8X4),
+                        lhsT_scale=h1s[:, g, t * P : (t + 1) * P],
+                        rhs=adjc[:, g * P : (g + 1) * P].bitcast(FP8X4),
+                        rhs_scale=adjs[:, g * P : (g + 1) * P],
+                        start=(g == 0),
+                        stop=(g == PASSES - 1),
+                    )
+            live[("aggp", i)] = aggp
+
+        def st_CA(i):
+            aggp = live[("aggp", i)]
+            aggg = rot3.tile([P, P, 4], BF16, align_bytes=64, tag="aggg")
+            nc.scalar.copy(out=aggg[:], in_=aggp[:].rearrange("p t i -> p i t"))
+            live[("aggg", i)] = aggg
+
+        def st_QA(i):
+            aggg = live[("aggg", i)]
+            aggc = rot3.tile([P, P], U32, align_bytes=64, tag="aggc")
+            aggs = rot3.tile([P, P], U8, align_bytes=64, tag="aggs")
+            nc.vector.quantize_mx(
+                out=aggc[:].bitcast(FP8X4), scales=aggs[:], in_=aggg[:].rearrange("p i t -> p (i t)")
+            )
+            live[("aggq", i)] = (aggc, aggs)
+
+        def st_N(i):
+            aggc, aggs = live[("aggq", i)]
+            linp = ps_lin.tile([P, FEAT], F32, tag="lin")
+            nc.tensor.matmul_mx(
+                out=linp[:],
+                lhsT=aggc[:].bitcast(FP8X4),
+                lhsT_scale=aggs[:],
+                rhs=w2c[:].bitcast(FP8X4),
+                rhs_scale=w2s[:],
+                start=True,
+                stop=True,
+            )
+            live[("linp", i)] = linp
+
+        def st_Y(i):
+            linp = live[("linp", i)]
+            y = rot4.tile([P, FEAT], F32, tag="y")
+            sumy = rot4.tile([P, 1], F32, tag="sumy")
+            mu = rot4.tile([P, 1], F32, tag="mu")
+            nc.vector.scalar_tensor_tensor(
+                out=y[:], in0=linp[:], scalar=1.0, in1=b2bc[:], op0=ALU.mult, op1=ALU.add, accum_out=sumy[:]
+            )
+            nc.vector.tensor_scalar(
+                out=mu[:], in0=sumy[:], scalar1=1.0 / FEAT, scalar2=None, op0=ALU.mult
+            )
+            live[("y", i)] = (y, mu)
+
+        def st_SQ(i):
+            y, mu = live[("y", i)]
+            junk = rot3.tile([P, FEAT], F32, tag="junk")
+            ss = rot4.tile([P, 1], F32, tag="ss")
+            nc.scalar.activation(
+                out=junk[:], in_=y[:], func=ACT.Square, bias=mu[:], scale=-1.0, accum_out=ss[:]
+            )
+            live[("ss", i)] = ss
+
+        def st_R(i):
+            ss = live[("ss", i)]
+            ve = rot4.tile([P, 1], F32, tag="ve")
+            rstd = rot4.tile([P, 1], F32, tag="rstd")
+            nc.gpsimd.tensor_scalar(
+                out=ve[:], in0=ss[:], scalar1=1.0 / FEAT, scalar2=LN_EPS, op0=ALU.mult, op1=ALU.add
+            )
+            nc.gpsimd.tensor_tensor(out=rstd[:], in0=ve[:], in1=neghalf[:], op=ALU.pow)
+            live[("rstd", i)] = rstd
+
+        def st_A(i):
+            y, mu = live[("y", i)]
+            t = rot6.tile([P, FEAT], F32, tag="t")
+            nc.vector.scalar_tensor_tensor(
+                out=t[:], in0=y[:], scalar=mu[:], in1=gbc[:], op0=ALU.subtract, op1=ALU.mult
+            )
+            live[("t", i)] = t
+
+        def st_B(i):
+            t = live[("t", i)]
+            rstd = live[("rstd", i)]
+            nc.vector.scalar_tensor_tensor(
+                out=t[:], in0=t[:], scalar=rstd[:], in1=betabc[:], op0=ALU.mult, op1=ALU.add
+            )
+
+        def st_GE(i):
+            t = live[("t", i)]
+            nc.scalar.activation(out=t[:], in_=t[:], func=ACT.Gelu)
+
+        def st_D(i):
+            t = live[("t", i)]
+            nc.gpsimd.tensor_tensor(out=t[:], in0=t[:], in1=res[i // 4][:, i % 4, :], op=ALU.add)
+
+        def st_ST(i):
+            t = live[("t", i)]
+            nc.sync.dma_start(out=out_t[i], in_=t[:])
+
+        stages = {
+            "T": st_T, "C": st_C, "Q": st_Q, "M": st_M, "CA": st_CA, "QA": st_QA, "N": st_N, "Y": st_Y,
+            "SQ": st_SQ, "R": st_R, "A": st_A, "B": st_B, "GE": st_GE, "D": st_D, "ST": st_ST,
+        }
+        depth = max(lag for name, lag in SCHED)
+        for s in range(TILES + depth):
+            if s == LEAD:
+                st_consts()
+                st_W()
+            for name, lag in SCHED:
+                if 0 <= s - lag < TILES:
+                    stages[name](s - lag)

@@ -39,9 +39,10 @@ def tile_multilayergnn_pb_kernel(tc, adj_norm, h1, W2, b2, g2, beta2, residual, 
         rot3 = ctx.enter_context(tc.tile_pool(name="rot3", bufs=3))
         rot4 = ctx.enter_context(tc.tile_pool(name="rot4", bufs=4))
         rot6 = ctx.enter_context(tc.tile_pool(name="rot6", bufs=6))
-        ps_tp = ctx.enter_context(tc.psum_pool(name="ps_tp", bufs=4))
+        ps_tp = ctx.enter_context(tc.psum_pool(name="ps_tp", bufs=2))
         ps_agg = ctx.enter_context(tc.psum_pool(name="ps_agg", bufs=2))
         ps_lin = ctx.enter_context(tc.psum_pool(name="ps_lin", bufs=2))
+        ps_const = ctx.enter_context(tc.psum_pool(name="ps_const", bufs=1))
         ctx.enter_context(tc.manual_schedule())
 
         adj_raw = [keep.tile([P, NODES], BF16, name="adj_raw%d" % i) for i in range(TILES)]
@@ -59,7 +60,9 @@ def tile_multilayergnn_pb_kernel(tc, adj_norm, h1, W2, b2, g2, beta2, residual, 
         identf = keep.tile([P, P], F32)
         identb = keep.tile([P, P], BF16)
         neghalf = keep.tile([P, 1], F32)
-        bcast = [keep.tile([P, FEAT], F32, name="bcast%d" % j) for j in range(3)]
+        b2bc = keep.tile([P, FEAT], F32)
+        gbc = ps_const.tile([P, FEAT], F32)
+        betabc = ps_const.tile([P, FEAT], F32)
 
         nc.vector.memset(cst[:], 0.0)
         nc.vector.memset(ones[:], 1.0)
@@ -109,12 +112,11 @@ def tile_multilayergnn_pb_kernel(tc, adj_norm, h1, W2, b2, g2, beta2, residual, 
         h1_quantise(PASSES - 1)
 
         def st_consts():
-            for j in range(3):
-                pb = ps_lin.tile([P, FEAT], F32, tag="lin")
-                nc.tensor.matmul(out=pb[:], lhsT=ones[:], rhs=cst[:, j, :], start=True, stop=True)
-                nc.scalar.copy(out=bcast[j][:], in_=pb[:])
-
-        b2bc, gbc, betabc = bcast
+            pb = ps_lin.tile([P, FEAT], F32, tag="lin")
+            nc.tensor.matmul(out=pb[:], lhsT=ones[:], rhs=cst[:, 0, :], start=True, stop=True)
+            nc.scalar.copy(out=b2bc[:], in_=pb[:])
+            nc.tensor.matmul(out=gbc[:], lhsT=ones[:], rhs=cst[:, 1, :], start=True, stop=True)
+            nc.tensor.matmul(out=betabc[:], lhsT=ones[:], rhs=cst[:, 2, :], start=True, stop=True)
 
         def st_W():
             for half in range(2):

@@ -20,16 +20,16 @@ LN_EPS = 1e-5
 
 FLOPS = 2 * NODES * NODES * FEAT + 2 * NODES * FEAT * FEAT
 
-LEAD = 2
 SCHED = (
-    ("GE", LEAD + 4), ("QA", LEAD + 1), ("T", 0), ("M", LEAD), ("N", LEAD + 1), ("Y", LEAD + 2),
-    ("A", LEAD + 2), ("B", LEAD + 3), ("C", 0), ("Q", 0), ("SQ", LEAD + 2), ("CA", LEAD),
-    ("D", LEAD + 4), ("R", LEAD + 2), ("ST", LEAD + 4),
+    ("Y", 5), ("SQ", 6), ("A", 6), ("D", 11), ("MU", 5), ("T", 0), ("Q", 1), ("B", 8), ("N", 4),
+    ("CA", 3), ("C", 0), ("QA", 3), ("GE", 10), ("R", 6), ("M", 2), ("ST", 11),
 )
 LOADS = (
-    "h0", "a0", "h1", "h2", "a1", "h3", "w", "a2", "a3", "a4", "a5", "a6", "a7", "a8", "r0",
+    "h0", "h1", "a0", "h2", "a1", "h3", "w", "a2", "a3", "a4", "a5", "a6", "a7", "a8", "r0",
     "a9", "a10", "a11", "a12", "r1", "a13", "a14", "a15", "r2", "r3",
 )
+ADD_ON_VECTOR = (13, 14, 15)
+FIRST_SINGLE = 14
 
 
 def tile_multilayergnn_pb_kernel(tc, adj_norm, h1, W2, b2, g2, beta2, residual, out):
@@ -38,8 +38,8 @@ def tile_multilayergnn_pb_kernel(tc, adj_norm, h1, W2, b2, g2, beta2, residual, 
         keep = ctx.enter_context(tc.tile_pool(name="keep", bufs=1))
         rot3 = ctx.enter_context(tc.tile_pool(name="rot3", bufs=3))
         rot4 = ctx.enter_context(tc.tile_pool(name="rot4", bufs=4))
-        rot6 = ctx.enter_context(tc.tile_pool(name="rot6", bufs=6))
-        ps_tp = ctx.enter_context(tc.psum_pool(name="ps_tp", bufs=2))
+        rot8 = ctx.enter_context(tc.tile_pool(name="rot8", bufs=8))
+        ps_tp = ctx.enter_context(tc.psum_pool(name="ps_tp", bufs=3))
         ps_agg = ctx.enter_context(tc.psum_pool(name="ps_agg", bufs=2))
         ps_lin = ctx.enter_context(tc.psum_pool(name="ps_lin", bufs=2))
         ps_const = ctx.enter_context(tc.psum_pool(name="ps_const", bufs=1))
@@ -59,10 +59,12 @@ def tile_multilayergnn_pb_kernel(tc, adj_norm, h1, W2, b2, g2, beta2, residual, 
         ones = keep.tile([P, P], BF16)
         identf = keep.tile([P, P], F32)
         identb = keep.tile([P, P], BF16)
-        neghalf = keep.tile([P, 1], F32)
+        neghalf = keep.tile([P, 2], F32)
         b2bc = keep.tile([P, FEAT], F32)
-        gbc = ps_const.tile([P, FEAT], F32)
-        betabc = ps_const.tile([P, FEAT], F32)
+        affine = ps_const.tile([P, 2, FEAT], BF16)
+        gbc = affine[:, 0, :]
+        betabc = affine[:, 1, :]
+        warm = keep.tile([P, 1], F32)
 
         nc.vector.memset(cst[:], 0.0)
         nc.vector.memset(ones[:], 1.0)
@@ -76,6 +78,7 @@ def tile_multilayergnn_pb_kernel(tc, adj_norm, h1, W2, b2, g2, beta2, residual, 
         out_t = out.rearrange("(a p) e -> a p e", p=P)
         for j, vec in enumerate((b2, g2, beta2)):
             nc.scalar.dma_start(out=cst[0:1, j, :], in_=vec.unsqueeze(0))
+        nc.scalar.activation(out=warm[:], in_=neghalf[:, 0:1], func=ACT.Gelu)
         for item in LOADS:
             kind = item[0]
             if kind == "a":
@@ -105,18 +108,12 @@ def tile_multilayergnn_pb_kernel(tc, adj_norm, h1, W2, b2, g2, beta2, residual, 
                 in_=h1g[:, g].rearrange("p h t -> p (h t)"),
             )
 
-        h1_regroup(0)
-        for g in range(1, PASSES):
-            h1_regroup(g)
-            h1_quantise(g - 1)
-        h1_quantise(PASSES - 1)
-
         def st_consts():
             pb = ps_lin.tile([P, FEAT], F32, tag="lin")
             nc.tensor.matmul(out=pb[:], lhsT=ones[:], rhs=cst[:, 0, :], start=True, stop=True)
             nc.scalar.copy(out=b2bc[:], in_=pb[:])
-            nc.tensor.matmul(out=gbc[:], lhsT=ones[:], rhs=cst[:, 1, :], start=True, stop=True)
-            nc.tensor.matmul(out=betabc[:], lhsT=ones[:], rhs=cst[:, 2, :], start=True, stop=True)
+            nc.tensor.matmul(out=gbc, lhsT=ones[:], rhs=cst[:, 1, :], start=True, stop=True)
+            nc.tensor.matmul(out=betabc, lhsT=ones[:], rhs=cst[:, 2, :], start=True, stop=True)
 
         def st_W():
             for half in range(2):
@@ -134,6 +131,11 @@ def tile_multilayergnn_pb_kernel(tc, adj_norm, h1, W2, b2, g2, beta2, residual, 
             )
 
         live = {}
+
+        def group(i):
+            if i >= FIRST_SINGLE:
+                return i, 1
+            return i - i % 2, 2
 
         def st_T(i):
             words = adj_raw[i][:].bitcast(F32)
@@ -213,10 +215,14 @@ def tile_multilayergnn_pb_kernel(tc, adj_norm, h1, W2, b2, g2, beta2, residual, 
             linp = live[("linp", i)]
             y = rot4.tile([P, FEAT], F32, tag="y")
             sumy = rot4.tile([P, 1], F32, tag="sumy")
-            mu = rot4.tile([P, 1], F32, tag="mu")
             nc.vector.scalar_tensor_tensor(
                 out=y[:], in0=linp[:], scalar=1.0, in1=b2bc[:], op0=ALU.mult, op1=ALU.add, accum_out=sumy[:]
             )
+            live[("sumy", i)] = (y, sumy)
+
+        def st_MU(i):
+            y, sumy = live[("sumy", i)]
+            mu = rot4.tile([P, 1], F32, tag="mu")
             nc.vector.tensor_scalar(
                 out=mu[:], in0=sumy[:], scalar1=1.0 / FEAT, scalar2=None, op0=ALU.mult
             )
@@ -225,35 +231,47 @@ def tile_multilayergnn_pb_kernel(tc, adj_norm, h1, W2, b2, g2, beta2, residual, 
         def st_SQ(i):
             y, mu = live[("y", i)]
             junk = rot3.tile([P, FEAT], F32, tag="junk")
-            ss = rot4.tile([P, 1], F32, tag="ss")
+            first, size = group(i)
+            if i == first:
+                ss = rot4.tile([P, 2], F32, tag="ss")
+                live[("ss", first)] = ss
+            ss = live[("ss", first)]
             nc.scalar.activation(
-                out=junk[:], in_=y[:], func=ACT.Square, bias=mu[:], scale=-1.0, accum_out=ss[:]
+                out=junk[:], in_=y[:], func=ACT.Square, bias=mu[:], scale=-1.0,
+                accum_out=ss[:, i - first : i - first + 1],
             )
-            live[("ss", i)] = ss
 
         def st_R(i):
-            ss = live[("ss", i)]
-            ve = rot4.tile([P, 1], F32, tag="ve")
-            rstd = rot4.tile([P, 1], F32, tag="rstd")
+            first, size = group(i)
+            if i != first + size - 1:
+                return
+            ss = live[("ss", first)]
+            ve = rot4.tile([P, 2], F32, tag="ve")
+            rstd = rot4.tile([P, 2], F32, tag="rstd")
             nc.gpsimd.tensor_scalar(
-                out=ve[:], in0=ss[:], scalar1=1.0 / FEAT, scalar2=LN_EPS, op0=ALU.mult, op1=ALU.add
+                out=ve[:, 0:size], in0=ss[:, 0:size], scalar1=1.0 / FEAT, scalar2=LN_EPS,
+                op0=ALU.mult, op1=ALU.add,
             )
-            nc.gpsimd.tensor_tensor(out=rstd[:], in0=ve[:], in1=neghalf[:], op=ALU.pow)
-            live[("rstd", i)] = rstd
+            nc.gpsimd.tensor_tensor(
+                out=rstd[:, 0:size], in0=ve[:, 0:size], in1=neghalf[:, 0:size], op=ALU.pow
+            )
+            live[("rstd", first)] = rstd
 
         def st_A(i):
             y, mu = live[("y", i)]
-            t = rot6.tile([P, FEAT], F32, tag="t")
+            t = rot8.tile([P, FEAT], F32, tag="t")
             nc.vector.scalar_tensor_tensor(
-                out=t[:], in0=y[:], scalar=mu[:], in1=gbc[:], op0=ALU.subtract, op1=ALU.mult
+                out=t[:], in0=y[:], scalar=mu[:], in1=gbc, op0=ALU.subtract, op1=ALU.mult
             )
             live[("t", i)] = t
 
         def st_B(i):
             t = live[("t", i)]
-            rstd = live[("rstd", i)]
+            first, size = group(i)
+            rstd = live[("rstd", first)]
             nc.vector.scalar_tensor_tensor(
-                out=t[:], in0=t[:], scalar=rstd[:], in1=betabc[:], op0=ALU.mult, op1=ALU.add
+                out=t[:], in0=t[:], scalar=rstd[:, i - first : i - first + 1], in1=betabc,
+                op0=ALU.mult, op1=ALU.add,
             )
 
         def st_GE(i):
@@ -262,21 +280,33 @@ def tile_multilayergnn_pb_kernel(tc, adj_norm, h1, W2, b2, g2, beta2, residual, 
 
         def st_D(i):
             t = live[("t", i)]
-            nc.gpsimd.tensor_tensor(out=t[:], in0=t[:], in1=res[i // 4][:, i % 4, :], op=ALU.add)
+            engine = nc.vector if i in ADD_ON_VECTOR else nc.gpsimd
+            engine.tensor_tensor(out=t[:], in0=t[:], in1=res[i // 4][:, i % 4, :], op=ALU.add)
 
         def st_ST(i):
             t = live[("t", i)]
             nc.sync.dma_start(out=out_t[i], in_=t[:])
 
         stages = {
-            "T": st_T, "C": st_C, "Q": st_Q, "M": st_M, "CA": st_CA, "QA": st_QA, "N": st_N, "Y": st_Y,
+            "T": st_T, "C": st_C, "Q": st_Q, "M": st_M, "CA": st_CA, "QA": st_QA, "N": st_N, "Y": st_Y, "MU": st_MU,
             "SQ": st_SQ, "R": st_R, "A": st_A, "B": st_B, "GE": st_GE, "D": st_D, "ST": st_ST,
         }
         depth = max(lag for name, lag in SCHED)
+        before = {
+            0: (lambda: h1_regroup(0), lambda: h1_regroup(1), lambda: h1_quantise(0)),
+            1: (lambda: h1_regroup(3), lambda: h1_quantise(2)),
+            2: (st_W,),
+            3: (st_consts,),
+        }
+        after = {
+            0: (lambda: h1_regroup(2), lambda: h1_quantise(1)),
+            1: (lambda: h1_quantise(3),),
+        }
         for s in range(TILES + depth):
-            if s == LEAD:
-                st_consts()
-                st_W()
+            for job in before.get(s, ()):
+                job()
             for name, lag in SCHED:
                 if 0 <= s - lag < TILES:
                     stages[name](s - lag)
+            for job in after.get(s, ()):
+                job()

@@ -17,19 +17,10 @@ FEAT = 512
 TILES = NODES // P
 PASSES = NODES // 512
 LN_EPS = 1e-5
+PIPELINE_DEPTH = 8
+FIRST_ADD_ON_VECTOR = 12
 
 FLOPS = 2 * NODES * NODES * FEAT + 2 * NODES * FEAT * FEAT
-
-SCHED = (
-    ("Y", 5), ("SQ", 6), ("A", 6), ("D", 11), ("MU", 5), ("T", 0), ("Q", 1), ("B", 8), ("N", 4),
-    ("CA", 3), ("C", 0), ("QA", 3), ("GE", 10), ("R", 6), ("M", 2), ("ST", 11),
-)
-LOADS = (
-    "h0", "h1", "a0", "h2", "a1", "h3", "w", "a2", "a3", "a4", "a5", "a6", "a7", "a8", "r0",
-    "a9", "a10", "a11", "a12", "r1", "a13", "a14", "a15", "r2", "r3",
-)
-ADD_ON_VECTOR = (13, 14, 15)
-FIRST_SINGLE = 14
 
 
 def tile_multilayergnn_pb_kernel(tc, adj_norm, h1, W2, b2, g2, beta2, residual, out):
@@ -38,7 +29,7 @@ def tile_multilayergnn_pb_kernel(tc, adj_norm, h1, W2, b2, g2, beta2, residual, 
         keep = ctx.enter_context(tc.tile_pool(name="keep", bufs=1))
         rot3 = ctx.enter_context(tc.tile_pool(name="rot3", bufs=3))
         rot4 = ctx.enter_context(tc.tile_pool(name="rot4", bufs=4))
-        rot8 = ctx.enter_context(tc.tile_pool(name="rot8", bufs=8))
+        rot6 = ctx.enter_context(tc.tile_pool(name="rot6", bufs=6))
         ps_tp = ctx.enter_context(tc.psum_pool(name="ps_tp", bufs=3))
         ps_agg = ctx.enter_context(tc.psum_pool(name="ps_agg", bufs=2))
         ps_lin = ctx.enter_context(tc.psum_pool(name="ps_lin", bufs=2))
@@ -55,18 +46,18 @@ def tile_multilayergnn_pb_kernel(tc, adj_norm, h1, W2, b2, g2, beta2, residual, 
         w2g = keep.tile([P, 4, P, 4], BF16, align_bytes=64)
         w2c = keep.tile([P, FEAT], U32, align_bytes=64)
         w2s = keep.tile([P, FEAT], U8, align_bytes=64)
-        cst = keep.tile([P, 3, FEAT], BF16)
+        vectors = keep.tile([P, 3, FEAT], BF16)
         ones = keep.tile([P, P], BF16)
         identf = keep.tile([P, P], F32)
         identb = keep.tile([P, P], BF16)
-        neghalf = keep.tile([P, 2], F32)
+        neghalf = keep.tile([P, 1], F32)
+        warm = keep.tile([P, 1], F32)
         b2bc = keep.tile([P, FEAT], F32)
         affine = ps_const.tile([P, 2, FEAT], BF16)
         gbc = affine[:, 0, :]
         betabc = affine[:, 1, :]
-        warm = keep.tile([P, 1], F32)
 
-        nc.vector.memset(cst[:], 0.0)
+        nc.vector.memset(vectors[:], 0.0)
         nc.vector.memset(ones[:], 1.0)
         nc.vector.memset(neghalf[:], -0.5)
         masks.make_identity(nc, identf[:])
@@ -76,24 +67,30 @@ def tile_multilayergnn_pb_kernel(tc, adj_norm, h1, W2, b2, g2, beta2, residual, 
         h1_t = h1.rearrange("(g u p e) h -> g p u (e h)", g=PASSES, u=2, p=P, e=2)
         res_t = residual.rearrange("(c a p) e -> c p a e", c=4, a=4, p=P)
         out_t = out.rearrange("(a p) e -> a p e", p=P)
+
+        def load_adj(i):
+            nc.sync.dma_start(out=adj_raw[i][:], in_=adj_t[i])
+
+        def load_h1(g):
+            nc.sync.dma_start(
+                out=h1raw[:, g].rearrange("p (u e) h -> p u (e h)", u=2, e=2), in_=h1_t[g]
+            )
+
         for j, vec in enumerate((b2, g2, beta2)):
-            nc.scalar.dma_start(out=cst[0:1, j, :], in_=vec.unsqueeze(0))
-        nc.scalar.activation(out=warm[:], in_=neghalf[:, 0:1], func=ACT.Gelu)
-        for item in LOADS:
-            kind = item[0]
-            if kind == "a":
-                i = int(item[1:])
-                nc.sync.dma_start(out=adj_raw[i][:], in_=adj_t[i])
-            elif kind == "h":
-                g = int(item[1:])
-                nc.sync.dma_start(
-                    out=h1raw[:, g].rearrange("p (u e) h -> p u (e h)", u=2, e=2), in_=h1_t[g]
-                )
-            elif kind == "r":
-                c = int(item[1:])
-                nc.sync.dma_start(out=res[c][:], in_=res_t[c])
-            else:
-                nc.sync.dma_start(out=w2raw[:], in_=W2.rearrange("(a p) h -> p a h", p=P))
+            nc.scalar.dma_start(out=vectors[0:1, j, :], in_=vec.unsqueeze(0))
+        nc.scalar.activation(out=warm[:], in_=neghalf[:], func=ACT.Gelu)
+        load_h1(0)
+        load_h1(1)
+        load_adj(0)
+        load_h1(2)
+        load_adj(1)
+        load_h1(3)
+        nc.sync.dma_start(out=w2raw[:], in_=W2.rearrange("(a p) h -> p a h", p=P))
+        for i in range(2, TILES):
+            load_adj(i)
+            if i % 4 == 0:
+                nc.sync.dma_start(out=res[i // 4 - 1][:], in_=res_t[i // 4 - 1])
+        nc.sync.dma_start(out=res[3][:], in_=res_t[3])
 
         def h1_regroup(g):
             nc.vector.tensor_copy(
@@ -108,14 +105,20 @@ def tile_multilayergnn_pb_kernel(tc, adj_norm, h1, W2, b2, g2, beta2, residual, 
                 in_=h1g[:, g].rearrange("p h t -> p (h t)"),
             )
 
-        def st_consts():
-            pb = ps_lin.tile([P, FEAT], F32, tag="lin")
-            nc.tensor.matmul(out=pb[:], lhsT=ones[:], rhs=cst[:, 0, :], start=True, stop=True)
-            nc.scalar.copy(out=b2bc[:], in_=pb[:])
-            nc.tensor.matmul(out=gbc, lhsT=ones[:], rhs=cst[:, 1, :], start=True, stop=True)
-            nc.tensor.matmul(out=betabc, lhsT=ones[:], rhs=cst[:, 2, :], start=True, stop=True)
+        h1_regroup(0)
+        for g in range(1, PASSES):
+            h1_regroup(g)
+            h1_quantise(g - 1)
+        h1_quantise(PASSES - 1)
 
-        def st_W():
+        def broadcast_vectors():
+            pb = ps_lin.tile([P, FEAT], F32, tag="lin")
+            nc.tensor.matmul(out=pb[:], lhsT=ones[:], rhs=vectors[:, 0, :], start=True, stop=True)
+            nc.scalar.copy(out=b2bc[:], in_=pb[:])
+            nc.tensor.matmul(out=gbc, lhsT=ones[:], rhs=vectors[:, 1, :], start=True, stop=True)
+            nc.tensor.matmul(out=betabc, lhsT=ones[:], rhs=vectors[:, 2, :], start=True, stop=True)
+
+        def prepare_w2():
             for half in range(2):
                 pw = ps_tp.tile([P, 2, 4, P], BF16, tag="tp")
                 for a in range(2):
@@ -132,12 +135,7 @@ def tile_multilayergnn_pb_kernel(tc, adj_norm, h1, W2, b2, g2, beta2, residual, 
 
         live = {}
 
-        def group(i):
-            if i >= FIRST_SINGLE:
-                return i, 1
-            return i - i % 2, 2
-
-        def st_T(i):
+        def transpose_adj(i):
             words = adj_raw[i][:].bitcast(F32)
             for b in range(2):
                 tp = ps_tp.tile([P, 2, 2, P], F32, tag="tp")
@@ -147,26 +145,27 @@ def tile_multilayergnn_pb_kernel(tc, adj_norm, h1, W2, b2, g2, beta2, residual, 
                         nc.tensor.transpose(tp[:, gg, u, :], words[:, w0 : w0 + P], identf[:])
                 live[("tp", i, b)] = tp
 
-        def st_C(i):
+        def copy_adj(i):
             adjg = rot3.tile([P, PASSES, P, 4], BF16, align_bytes=64, tag="adjg")
             adjgf = adjg[:].bitcast(F32)
             for b in range(2):
-                tp = live[("tp", i, b)]
                 nc.scalar.copy(
-                    out=adjgf[:, 2 * b : 2 * b + 2], in_=tp[:].rearrange("p g u i -> p g i u")
+                    out=adjgf[:, 2 * b : 2 * b + 2],
+                    in_=live[("tp", i, b)][:].rearrange("p g u i -> p g i u"),
                 )
             live[("adjg", i)] = adjg
 
-        def st_Q(i):
-            adjg = live[("adjg", i)]
+        def quantise_adj(i):
             adjc = rot4.tile([P, PASSES * P], U32, align_bytes=64, tag="adjc")
             adjs = rot4.tile([P, PASSES * P], U8, align_bytes=64, tag="adjs")
             nc.vector.quantize_mx(
-                out=adjc[:].bitcast(FP8X4), scales=adjs[:], in_=adjg[:].rearrange("p g i t -> p (g i t)")
+                out=adjc[:].bitcast(FP8X4),
+                scales=adjs[:],
+                in_=live[("adjg", i)][:].rearrange("p g i t -> p (g i t)"),
             )
             live[("adjq", i)] = (adjc, adjs)
 
-        def st_M(i):
+        def first_matmul(i):
             adjc, adjs = live[("adjq", i)]
             aggp = ps_agg.tile([P, 4, P], F32, tag="agg")
             for t in range(4):
@@ -182,22 +181,22 @@ def tile_multilayergnn_pb_kernel(tc, adj_norm, h1, W2, b2, g2, beta2, residual, 
                     )
             live[("aggp", i)] = aggp
 
-        def st_CA(i):
-            aggp = live[("aggp", i)]
+        def copy_agg(i):
             aggg = rot3.tile([P, P, 4], BF16, align_bytes=64, tag="aggg")
-            nc.scalar.copy(out=aggg[:], in_=aggp[:].rearrange("p t i -> p i t"))
+            nc.scalar.copy(out=aggg[:], in_=live[("aggp", i)][:].rearrange("p t i -> p i t"))
             live[("aggg", i)] = aggg
 
-        def st_QA(i):
-            aggg = live[("aggg", i)]
+        def quantise_agg(i):
             aggc = rot3.tile([P, P], U32, align_bytes=64, tag="aggc")
             aggs = rot3.tile([P, P], U8, align_bytes=64, tag="aggs")
             nc.vector.quantize_mx(
-                out=aggc[:].bitcast(FP8X4), scales=aggs[:], in_=aggg[:].rearrange("p i t -> p (i t)")
+                out=aggc[:].bitcast(FP8X4),
+                scales=aggs[:],
+                in_=live[("aggg", i)][:].rearrange("p i t -> p (i t)"),
             )
             live[("aggq", i)] = (aggc, aggs)
 
-        def st_N(i):
+        def second_matmul(i):
             aggc, aggs = live[("aggq", i)]
             linp = ps_lin.tile([P, FEAT], F32, tag="lin")
             nc.tensor.matmul_mx(
@@ -211,102 +210,91 @@ def tile_multilayergnn_pb_kernel(tc, adj_norm, h1, W2, b2, g2, beta2, residual, 
             )
             live[("linp", i)] = linp
 
-        def st_Y(i):
-            linp = live[("linp", i)]
+        def add_bias(i):
             y = rot4.tile([P, FEAT], F32, tag="y")
             sumy = rot4.tile([P, 1], F32, tag="sumy")
             nc.vector.scalar_tensor_tensor(
-                out=y[:], in0=linp[:], scalar=1.0, in1=b2bc[:], op0=ALU.mult, op1=ALU.add, accum_out=sumy[:]
+                out=y[:], in0=live[("linp", i)][:], scalar=1.0, in1=b2bc[:],
+                op0=ALU.mult, op1=ALU.add, accum_out=sumy[:],
             )
-            live[("sumy", i)] = (y, sumy)
+            live[("y", i)] = y
+            live[("sumy", i)] = sumy
 
-        def st_MU(i):
-            y, sumy = live[("sumy", i)]
+        def mean(i):
             mu = rot4.tile([P, 1], F32, tag="mu")
             nc.vector.tensor_scalar(
-                out=mu[:], in0=sumy[:], scalar1=1.0 / FEAT, scalar2=None, op0=ALU.mult
+                out=mu[:], in0=live[("sumy", i)][:], scalar1=1.0 / FEAT, scalar2=None, op0=ALU.mult
             )
-            live[("y", i)] = (y, mu)
+            live[("mu", i)] = mu
 
-        def st_SQ(i):
-            y, mu = live[("y", i)]
+        def sum_squares(i):
             junk = rot3.tile([P, FEAT], F32, tag="junk")
-            first, size = group(i)
-            if i == first:
-                ss = rot4.tile([P, 2], F32, tag="ss")
-                live[("ss", first)] = ss
-            ss = live[("ss", first)]
+            ss = rot4.tile([P, 1], F32, tag="ss")
             nc.scalar.activation(
-                out=junk[:], in_=y[:], func=ACT.Square, bias=mu[:], scale=-1.0,
-                accum_out=ss[:, i - first : i - first + 1],
+                out=junk[:], in_=live[("y", i)][:], func=ACT.Square, bias=live[("mu", i)][:],
+                scale=-1.0, accum_out=ss[:],
             )
+            live[("ss", i)] = ss
 
-        def st_R(i):
-            first, size = group(i)
-            if i != first + size - 1:
-                return
-            ss = live[("ss", first)]
-            ve = rot4.tile([P, 2], F32, tag="ve")
-            rstd = rot4.tile([P, 2], F32, tag="rstd")
+        def inverse_std(i):
+            ve = rot4.tile([P, 1], F32, tag="ve")
+            rstd = rot4.tile([P, 1], F32, tag="rstd")
             nc.gpsimd.tensor_scalar(
-                out=ve[:, 0:size], in0=ss[:, 0:size], scalar1=1.0 / FEAT, scalar2=LN_EPS,
+                out=ve[:], in0=live[("ss", i)][:], scalar1=1.0 / FEAT, scalar2=LN_EPS,
                 op0=ALU.mult, op1=ALU.add,
             )
-            nc.gpsimd.tensor_tensor(
-                out=rstd[:, 0:size], in0=ve[:, 0:size], in1=neghalf[:, 0:size], op=ALU.pow
-            )
-            live[("rstd", first)] = rstd
+            nc.gpsimd.tensor_tensor(out=rstd[:], in0=ve[:], in1=neghalf[:], op=ALU.pow)
+            live[("rstd", i)] = rstd
 
-        def st_A(i):
-            y, mu = live[("y", i)]
-            t = rot8.tile([P, FEAT], F32, tag="t")
+        def centre_and_gain(i):
+            t = rot6.tile([P, FEAT], F32, tag="t")
             nc.vector.scalar_tensor_tensor(
-                out=t[:], in0=y[:], scalar=mu[:], in1=gbc, op0=ALU.subtract, op1=ALU.mult
+                out=t[:], in0=live[("y", i)][:], scalar=live[("mu", i)][:], in1=gbc,
+                op0=ALU.subtract, op1=ALU.mult,
             )
             live[("t", i)] = t
 
-        def st_B(i):
+        def scale_and_shift(i):
             t = live[("t", i)]
-            first, size = group(i)
-            rstd = live[("rstd", first)]
             nc.vector.scalar_tensor_tensor(
-                out=t[:], in0=t[:], scalar=rstd[:, i - first : i - first + 1], in1=betabc,
+                out=t[:], in0=t[:], scalar=live[("rstd", i)][:], in1=betabc,
                 op0=ALU.mult, op1=ALU.add,
             )
 
-        def st_GE(i):
+        def gelu(i):
             t = live[("t", i)]
             nc.scalar.activation(out=t[:], in_=t[:], func=ACT.Gelu)
 
-        def st_D(i):
+        def add_residual(i):
             t = live[("t", i)]
-            engine = nc.vector if i in ADD_ON_VECTOR else nc.gpsimd
+            engine = nc.vector if i >= FIRST_ADD_ON_VECTOR else nc.gpsimd
             engine.tensor_tensor(out=t[:], in0=t[:], in1=res[i // 4][:, i % 4, :], op=ALU.add)
 
-        def st_ST(i):
-            t = live[("t", i)]
-            nc.sync.dma_start(out=out_t[i], in_=t[:])
+        def store(i):
+            nc.sync.dma_start(out=out_t[i], in_=live[("t", i)][:])
 
-        stages = {
-            "T": st_T, "C": st_C, "Q": st_Q, "M": st_M, "CA": st_CA, "QA": st_QA, "N": st_N, "Y": st_Y, "MU": st_MU,
-            "SQ": st_SQ, "R": st_R, "A": st_A, "B": st_B, "GE": st_GE, "D": st_D, "ST": st_ST,
-        }
-        depth = max(lag for name, lag in SCHED)
-        before = {
-            0: (lambda: h1_regroup(0), lambda: h1_regroup(1), lambda: h1_quantise(0)),
-            1: (lambda: h1_regroup(3), lambda: h1_quantise(2)),
-            2: (st_W,),
-            3: (st_consts,),
-        }
-        after = {
-            0: (lambda: h1_regroup(2), lambda: h1_quantise(1)),
-            1: (lambda: h1_quantise(3),),
-        }
-        for s in range(TILES + depth):
-            for job in before.get(s, ()):
-                job()
-            for name, lag in SCHED:
-                if 0 <= s - lag < TILES:
-                    stages[name](s - lag)
-            for job in after.get(s, ()):
-                job()
+        def at(stage, i):
+            if 0 <= i < TILES:
+                stage(i)
+
+        for s in range(TILES + PIPELINE_DEPTH):
+            if s == 2:
+                prepare_w2()
+            if s == 3:
+                broadcast_vectors()
+            at(copy_agg, s - 3)
+            at(quantise_agg, s - 3)
+            at(quantise_adj, s - 1)
+            at(transpose_adj, s)
+            at(second_matmul, s - 4)
+            at(first_matmul, s - 2)
+            at(sum_squares, s - 6)
+            at(add_bias, s - 5)
+            at(centre_and_gain, s - 6)
+            at(mean, s - 5)
+            at(scale_and_shift, s - 7)
+            at(gelu, s - 8)
+            at(add_residual, s - 8)
+            at(copy_adj, s)
+            at(inverse_std, s - 6)
+            at(store, s - 8)

@@ -18,7 +18,7 @@ TILES = NODES // P
 PASSES = NODES // 512
 LN_EPS = 1e-5
 PIPELINE_DEPTH = 8
-FIRST_ADD_ON_VECTOR = 12
+FIRST_ADD_ON_VECTOR = 0
 
 FLOPS = 2 * NODES * NODES * FEAT + 2 * NODES * FEAT * FEAT
 

@@ -18,7 +18,7 @@ TILES = NODES // P
 PASSES = NODES // 512
 LN_EPS = 1e-5
 PIPELINE_DEPTH = 8
-FIRST_ADD_ON_VECTOR = 0
+FIRST_ADD_ON_VECTOR = 12
 
 FLOPS = 2 * NODES * NODES * FEAT + 2 * NODES * FEAT * FEAT
 
@@ -34,7 +34,6 @@ def tile_multilayergnn_pb_kernel(tc, adj_norm, h1, W2, b2, g2, beta2, residual, 
         ps_agg = ctx.enter_context(tc.psum_pool(name="ps_agg", bufs=2))
         ps_lin = ctx.enter_context(tc.psum_pool(name="ps_lin", bufs=2))
         ps_const = ctx.enter_context(tc.psum_pool(name="ps_const", bufs=1))
-        ctx.enter_context(tc.manual_schedule())
 
         adj_raw = [keep.tile([P, NODES], BF16, name="adj_raw%d" % i) for i in range(TILES)]
         res = [keep.tile([P, 4, FEAT], BF16, name="res%d" % c) for c in range(4)]

@@ -76,7 +76,7 @@ def tile_multilayergnn_pb_kernel(tc, adj_norm, h1, W2, b2, g2, beta2, residual, 
             )
 
         for j, vec in enumerate((b2, g2, beta2)):
-            nc.scalar.dma_start(out=vectors[0:1, j, :], in_=vec.unsqueeze(0))
+            nc.sync.dma_start(out=vectors[0:1, j, :], in_=vec.unsqueeze(0))
         nc.scalar.activation(out=warm[:], in_=neghalf[:], func=ACT.Gelu)
         load_h1(0)
         load_h1(1)

@@ -17,7 +17,6 @@ FEAT = 512
 TILES = NODES // P
 PASSES = NODES // 512
 LN_EPS = 1e-5
-PIPELINE_DEPTH = 8
 FIRST_ADD_ON_VECTOR = 12
 
 FLOPS = 2 * NODES * NODES * FEAT + 2 * NODES * FEAT * FEAT
@@ -75,8 +74,10 @@ def tile_multilayergnn_pb_kernel(tc, adj_norm, h1, W2, b2, g2, beta2, residual, 
                 out=h1raw[:, g].rearrange("p (u e) h -> p u (e h)", u=2, e=2), in_=h1_t[g]
             )
 
-        for j, vec in enumerate((b2, g2, beta2)):
-            nc.sync.dma_start(out=vectors[0:1, j, :], in_=vec.unsqueeze(0))
+        def load_vectors():
+            for j, vec in enumerate((b2, g2, beta2)):
+                nc.sync.dma_start(out=vectors[0:1, j, :], in_=vec.unsqueeze(0))
+
         nc.scalar.activation(out=warm[:], in_=neghalf[:], func=ACT.Gelu)
         load_h1(0)
         load_h1(1)
@@ -85,10 +86,24 @@ def tile_multilayergnn_pb_kernel(tc, adj_norm, h1, W2, b2, g2, beta2, residual, 
         load_adj(1)
         load_h1(3)
         nc.sync.dma_start(out=w2raw[:], in_=W2.rearrange("(a p) h -> p a h", p=P))
-        for i in range(2, TILES):
-            load_adj(i)
-            if i % 4 == 0:
-                nc.sync.dma_start(out=res[i // 4 - 1][:], in_=res_t[i // 4 - 1])
+        load_vectors()
+        load_adj(2)
+        load_adj(3)
+        load_adj(4)
+        nc.sync.dma_start(out=res[0][:], in_=res_t[0])
+        load_adj(5)
+        load_adj(6)
+        load_adj(7)
+        load_adj(8)
+        nc.sync.dma_start(out=res[1][:], in_=res_t[1])
+        load_adj(9)
+        load_adj(10)
+        load_adj(11)
+        load_adj(12)
+        nc.sync.dma_start(out=res[2][:], in_=res_t[2])
+        load_adj(13)
+        load_adj(14)
+        load_adj(15)
         nc.sync.dma_start(out=res[3][:], in_=res_t[3])
 
         def h1_regroup(g):
@@ -103,12 +118,6 @@ def tile_multilayergnn_pb_kernel(tc, adj_norm, h1, W2, b2, g2, beta2, residual, 
                 scales=h1s[:, g],
                 in_=h1g[:, g].rearrange("p h t -> p (h t)"),
             )
-
-        h1_regroup(0)
-        for g in range(1, PASSES):
-            h1_regroup(g)
-            h1_quantise(g - 1)
-        h1_quantise(PASSES - 1)
 
         def broadcast_vectors():
             pb = ps_lin.tile([P, FEAT], F32, tag="lin")
@@ -128,6 +137,8 @@ def tile_multilayergnn_pb_kernel(tc, adj_norm, h1, W2, b2, g2, beta2, residual, 
                 nc.scalar.copy(
                     out=w2g[:, 2 * half : 2 * half + 2], in_=pw[:].rearrange("p a t e -> p a e t")
                 )
+
+        def quantise_w2():
             nc.vector.quantize_mx(
                 out=w2c[:].bitcast(FP8X4), scales=w2s[:], in_=w2g[:].rearrange("p a e t -> p (a e t)")
             )
@@ -276,24 +287,43 @@ def tile_multilayergnn_pb_kernel(tc, adj_norm, h1, W2, b2, g2, beta2, residual, 
             if 0 <= i < TILES:
                 stage(i)
 
-        for s in range(TILES + PIPELINE_DEPTH):
-            if s == 2:
-                prepare_w2()
-            if s == 3:
-                broadcast_vectors()
-            at(copy_agg, s - 3)
-            at(quantise_agg, s - 3)
-            at(quantise_adj, s - 1)
-            at(transpose_adj, s)
-            at(second_matmul, s - 4)
-            at(first_matmul, s - 2)
-            at(sum_squares, s - 6)
-            at(add_bias, s - 5)
-            at(centre_and_gain, s - 6)
-            at(mean, s - 5)
-            at(scale_and_shift, s - 7)
-            at(gelu, s - 8)
-            at(add_residual, s - 8)
-            at(copy_adj, s)
-            at(inverse_std, s - 6)
-            at(store, s - 8)
+        with tc.manual_schedule():
+            for s in range(TILES + 7):
+                if s == 0:
+                    h1_regroup(0)
+                if s == 0:
+                    h1_regroup(1)
+                if s == 0:
+                    h1_quantise(0)
+                if s == 1:
+                    h1_regroup(2)
+                if s == 1:
+                    h1_quantise(1)
+                if s == 2:
+                    h1_regroup(3)
+                if s == 2:
+                    h1_quantise(2)
+                if s == 2:
+                    h1_quantise(3)
+                if s == 2:
+                    prepare_w2()
+                if s == 2:
+                    quantise_w2()
+                if s == 2:
+                    broadcast_vectors()
+                at(centre_and_gain, s - 4)
+                at(transpose_adj, s - 0)
+                at(copy_adj, s - 0)
+                at(first_matmul, s - 2)
+                at(copy_agg, s - 2)
+                at(second_matmul, s - 3)
+                at(sum_squares, s - 4)
+                at(add_bias, s - 3)
+                at(quantise_adj, s - 0)
+                at(mean, s - 3)
+                at(gelu, s - 6)
+                at(quantise_agg, s - 2)
+                at(scale_and_shift, s - 5)
+                at(add_residual, s - 7)
+                at(store, s - 7)
+                at(inverse_std, s - 4)

@@ -48,7 +48,7 @@ def tile_multilayergnn_pb_kernel(tc, adj_norm, h1, W2, b2, g2, beta2, residual, 
         ones = keep.tile([P, P], BF16)
         identf = keep.tile([P, P], F32)
         identb = keep.tile([P, P], BF16)
-        neghalf = keep.tile([P, 1], F32)
+        neghalf = keep.tile([P, 2], F32)
         warm = keep.tile([P, 1], F32)
         b2bc = keep.tile([P, FEAT], F32)
         affine = ps_const.tile([P, 2, FEAT], BF16)
@@ -78,15 +78,15 @@ def tile_multilayergnn_pb_kernel(tc, adj_norm, h1, W2, b2, g2, beta2, residual, 
             for j, vec in enumerate((b2, g2, beta2)):
                 nc.sync.dma_start(out=vectors[0:1, j, :], in_=vec.unsqueeze(0))
 
-        nc.scalar.activation(out=warm[:], in_=neghalf[:], func=ACT.Gelu)
+        nc.scalar.activation(out=warm[:], in_=neghalf[:, 0:1], func=ACT.Gelu)
         load_h1(0)
         load_h1(1)
-        load_adj(0)
         load_h1(2)
+        load_vectors()
+        load_adj(0)
         load_adj(1)
         load_h1(3)
         nc.sync.dma_start(out=w2raw[:], in_=W2.rearrange("(a p) h -> p a h", p=P))
-        load_vectors()
         load_adj(2)
         load_adj(3)
         load_adj(4)
@@ -239,22 +239,26 @@ def tile_multilayergnn_pb_kernel(tc, adj_norm, h1, W2, b2, g2, beta2, residual, 
 
         def sum_squares(i):
             junk = rot3.tile([P, FEAT], F32, tag="junk")
-            ss = rot4.tile([P, 1], F32, tag="ss")
+            if i % 2 == 0:
+                live[("ss2", i // 2)] = rot4.tile([P, 2], F32, name="ss", tag="ss")
+            ss = live[("ss2", i // 2)][:, i % 2 : i % 2 + 1]
             nc.scalar.activation(
                 out=junk[:], in_=live[("y", i)][:], func=ACT.Square, bias=live[("mu", i)][:],
-                scale=-1.0, accum_out=ss[:],
+                scale=-1.0, accum_out=ss,
             )
-            live[("ss", i)] = ss
 
         def inverse_std(i):
-            ve = rot4.tile([P, 1], F32, tag="ve")
-            rstd = rot4.tile([P, 1], F32, tag="rstd")
+            if i % 2 == 0:
+                return
+            ve = rot4.tile([P, 2], F32, tag="ve")
+            rstd = rot4.tile([P, 2], F32, tag="rstd")
             nc.gpsimd.tensor_scalar(
-                out=ve[:], in0=live[("ss", i)][:], scalar1=1.0 / FEAT, scalar2=LN_EPS,
+                out=ve[:], in0=live[("ss2", i // 2)][:], scalar1=1.0 / FEAT, scalar2=LN_EPS,
                 op0=ALU.mult, op1=ALU.add,
             )
             nc.gpsimd.tensor_tensor(out=rstd[:], in0=ve[:], in1=neghalf[:], op=ALU.pow)
-            live[("rstd", i)] = rstd
+            live[("rstd", i - 1)] = rstd[:, 0:1]
+            live[("rstd", i)] = rstd[:, 1:2]
 
         def centre_and_gain(i):
             t = rot6.tile([P, FEAT], F32, tag="t")
@@ -267,7 +271,7 @@ def tile_multilayergnn_pb_kernel(tc, adj_norm, h1, W2, b2, g2, beta2, residual, 
         def scale_and_shift(i):
             t = live[("t", i)]
             nc.vector.scalar_tensor_tensor(
-                out=t[:], in0=t[:], scalar=live[("rstd", i)][:], in1=betabc,
+                out=t[:], in0=t[:], scalar=live[("rstd", i)], in1=betabc,
                 op0=ALU.mult, op1=ALU.add,
             )
 
@@ -288,42 +292,42 @@ def tile_multilayergnn_pb_kernel(tc, adj_norm, h1, W2, b2, g2, beta2, residual, 
                 stage(i)
 
         with tc.manual_schedule():
-            for s in range(TILES + 7):
+            for s in range(TILES + 12):
                 if s == 0:
                     h1_regroup(0)
                 if s == 0:
                     h1_regroup(1)
                 if s == 0:
                     h1_quantise(0)
-                if s == 1:
+                if s == 0:
                     h1_regroup(2)
-                if s == 1:
+                if s == 0:
                     h1_quantise(1)
-                if s == 2:
+                if s == 1:
                     h1_regroup(3)
-                if s == 2:
+                if s == 1:
                     h1_quantise(2)
-                if s == 2:
-                    h1_quantise(3)
+                if s == 1:
+                    broadcast_vectors()
                 if s == 2:
                     prepare_w2()
                 if s == 2:
+                    h1_quantise(3)
+                if s == 3:
                     quantise_w2()
-                if s == 2:
-                    broadcast_vectors()
-                at(centre_and_gain, s - 4)
+                at(second_matmul, s - 4)
+                at(add_residual, s - 11)
+                at(store, s - 12)
+                at(add_bias, s - 4)
+                at(quantise_adj, s - 1)
+                at(quantise_agg, s - 3)
+                at(inverse_std, s - 6)
+                at(mean, s - 4)
+                at(centre_and_gain, s - 5)
                 at(transpose_adj, s - 0)
-                at(copy_adj, s - 0)
+                at(scale_and_shift, s - 7)
                 at(first_matmul, s - 2)
+                at(gelu, s - 9)
+                at(copy_adj, s - 0)
                 at(copy_agg, s - 2)
-                at(second_matmul, s - 3)
                 at(sum_squares, s - 4)
-                at(add_bias, s - 3)
-                at(quantise_adj, s - 0)
-                at(mean, s - 3)
-                at(gelu, s - 6)
-                at(quantise_agg, s - 2)
-                at(scale_and_shift, s - 5)
-                at(add_residual, s - 7)
-                at(store, s - 7)
-                at(inverse_std, s - 4)

@@ -26,9 +26,9 @@ def tile_multilayergnn_pb_kernel(tc, adj_norm, h1, W2, b2, g2, beta2, residual, 
     nc = tc.nc
     with ExitStack() as ctx:
         keep = ctx.enter_context(tc.tile_pool(name="keep", bufs=1))
-        rot3 = ctx.enter_context(tc.tile_pool(name="rot3", bufs=3))
-        rot4 = ctx.enter_context(tc.tile_pool(name="rot4", bufs=4))
-        rot6 = ctx.enter_context(tc.tile_pool(name="rot6", bufs=6))
+        rot3 = ctx.enter_context(tc.tile_pool(name="rot3", bufs=4))
+        rot4 = ctx.enter_context(tc.tile_pool(name="rot4", bufs=6))
+        rot6 = ctx.enter_context(tc.tile_pool(name="rot6", bufs=12))
         ps_tp = ctx.enter_context(tc.psum_pool(name="ps_tp", bufs=3))
         ps_agg = ctx.enter_context(tc.psum_pool(name="ps_agg", bufs=2))
         ps_lin = ctx.enter_context(tc.psum_pool(name="ps_lin", bufs=2))
@@ -82,10 +82,10 @@ def tile_multilayergnn_pb_kernel(tc, adj_norm, h1, W2, b2, g2, beta2, residual, 
         load_h1(0)
         load_h1(1)
         load_h1(2)
-        load_vectors()
         load_adj(0)
-        load_adj(1)
         load_h1(3)
+        load_vectors()
+        load_adj(1)
         nc.sync.dma_start(out=w2raw[:], in_=W2.rearrange("(a p) h -> p a h", p=P))
         load_adj(2)
         load_adj(3)
@@ -119,6 +119,11 @@ def tile_multilayergnn_pb_kernel(tc, adj_norm, h1, W2, b2, g2, beta2, residual, 
                 in_=h1g[:, g].rearrange("p h t -> p (h t)"),
             )
 
+        def keep_clock(source, count):
+            for _ in range(count):
+                scrap = ps_lin.tile([P, FEAT], F32, name="scrap", tag="lin")
+                nc.tensor.matmul(out=scrap[:], lhsT=identb[:], rhs=source, start=True, stop=True)
+
         def broadcast_vectors():
             pb = ps_lin.tile([P, FEAT], F32, tag="lin")
             nc.tensor.matmul(out=pb[:], lhsT=ones[:], rhs=vectors[:, 0, :], start=True, stop=True)
@@ -145,25 +150,36 @@ def tile_multilayergnn_pb_kernel(tc, adj_norm, h1, W2, b2, g2, beta2, residual, 
 
         live = {}
 
-        def transpose_adj(i):
+        def transpose_half(i, b):
             words = adj_raw[i][:].bitcast(F32)
-            for b in range(2):
-                tp = ps_tp.tile([P, 2, 2, P], F32, tag="tp")
-                for gg in range(2):
-                    for u in range(2):
-                        w0 = 256 * (2 * b + gg) + P * u
-                        nc.tensor.transpose(tp[:, gg, u, :], words[:, w0 : w0 + P], identf[:])
-                live[("tp", i, b)] = tp
+            tp = ps_tp.tile([P, 2, 2, P], F32, tag="tp")
+            for gg in range(2):
+                for u in range(2):
+                    w0 = 256 * (2 * b + gg) + P * u
+                    nc.tensor.transpose(tp[:, gg, u, :], words[:, w0 : w0 + P], identf[:])
+            live[("tp", i, b)] = tp
 
-        def copy_adj(i):
-            adjg = rot3.tile([P, PASSES, P, 4], BF16, align_bytes=64, tag="adjg")
-            adjgf = adjg[:].bitcast(F32)
-            for b in range(2):
-                nc.scalar.copy(
-                    out=adjgf[:, 2 * b : 2 * b + 2],
-                    in_=live[("tp", i, b)][:].rearrange("p g u i -> p g i u"),
-                )
-            live[("adjg", i)] = adjg
+        def copy_half(i, b):
+            if b == 0:
+                live[("adjg", i)] = rot3.tile([P, PASSES, P, 4], BF16, name="adjg", align_bytes=64, tag="adjg")
+            adjgf = live[("adjg", i)][:].bitcast(F32)
+            source = live[("tp", i, b)][:].rearrange("p g u i -> p g i u")
+            if b == 1 and (False):
+                nc.vector.tensor_copy(out=adjgf[:, 2 * b : 2 * b + 2], in_=source)
+            else:
+                nc.scalar.copy(out=adjgf[:, 2 * b : 2 * b + 2], in_=source)
+
+        def transpose0(i):
+            transpose_half(i, 0)
+
+        def transpose1(i):
+            transpose_half(i, 1)
+
+        def copy0(i):
+            copy_half(i, 0)
+
+        def copy1(i):
+            copy_half(i, 1)
 
         def quantise_adj(i):
             adjc = rot4.tile([P, PASSES * P], U32, align_bytes=64, tag="adjc")
@@ -248,17 +264,19 @@ def tile_multilayergnn_pb_kernel(tc, adj_norm, h1, W2, b2, g2, beta2, residual, 
             )
 
         def inverse_std(i):
-            if i % 2 == 0:
+            first = i if i >= TILES - 2 else i - 1
+            if first % 2 == 1 and i < TILES - 2 or first < 0:
                 return
+            cols = slice(first % 2, i % 2 + 1)
             ve = rot4.tile([P, 2], F32, tag="ve")
             rstd = rot4.tile([P, 2], F32, tag="rstd")
             nc.gpsimd.tensor_scalar(
-                out=ve[:], in0=live[("ss2", i // 2)][:], scalar1=1.0 / FEAT, scalar2=LN_EPS,
+                out=ve[:, cols], in0=live[("ss2", i // 2)][:, cols], scalar1=1.0 / FEAT, scalar2=LN_EPS,
                 op0=ALU.mult, op1=ALU.add,
             )
-            nc.gpsimd.tensor_tensor(out=rstd[:], in0=ve[:], in1=neghalf[:], op=ALU.pow)
-            live[("rstd", i - 1)] = rstd[:, 0:1]
-            live[("rstd", i)] = rstd[:, 1:2]
+            nc.gpsimd.tensor_tensor(out=rstd[:, cols], in0=ve[:, cols], in1=neghalf[:, cols], op=ALU.pow)
+            for j in range(first, i + 1):
+                live[("rstd", j)] = rstd[:, j % 2 : j % 2 + 1]
 
         def centre_and_gain(i):
             t = rot6.tile([P, FEAT], F32, tag="t")
@@ -279,20 +297,25 @@ def tile_multilayergnn_pb_kernel(tc, adj_norm, h1, W2, b2, g2, beta2, residual, 
             t = live[("t", i)]
             nc.scalar.activation(out=t[:], in_=t[:], func=ACT.Gelu)
 
-        def add_residual(i):
-            t = live[("t", i)]
-            engine = nc.vector if i >= FIRST_ADD_ON_VECTOR else nc.gpsimd
-            engine.tensor_tensor(out=t[:], in0=t[:], in1=res[i // 4][:, i % 4, :], op=ALU.add)
+        def add_residual(engine, i):
+            t = live[("t", i)][:]
+            engine.tensor_tensor(out=t, in0=t, in1=res[i // 4][:, i % 4, :], op=ALU.add)
+            nc.sync.dma_start(out=out_t[i], in_=t)
 
-        def store(i):
-            nc.sync.dma_start(out=out_t[i], in_=live[("t", i)][:])
+        def add_gpsimd(i):
+            if i < FIRST_ADD_ON_VECTOR:
+                add_residual(nc.gpsimd, i)
+
+        def add_vector(i):
+            if i >= FIRST_ADD_ON_VECTOR:
+                add_residual(nc.vector, i)
 
         def at(stage, i):
             if 0 <= i < TILES:
                 stage(i)
 
         with tc.manual_schedule():
-            for s in range(TILES + 12):
+            for s in range(TILES + 10):
                 if s == 0:
                     h1_regroup(0)
                 if s == 0:
@@ -303,6 +326,10 @@ def tile_multilayergnn_pb_kernel(tc, adj_norm, h1, W2, b2, g2, beta2, residual, 
                     h1_regroup(2)
                 if s == 0:
                     h1_quantise(1)
+                if s == 0:
+                    keep_clock(h1raw[:, 1, 0, :], 2)
+                if s == 0:
+                    keep_clock(h1raw[:, 2, 0, :], 2)
                 if s == 1:
                     h1_regroup(3)
                 if s == 1:
@@ -310,24 +337,30 @@ def tile_multilayergnn_pb_kernel(tc, adj_norm, h1, W2, b2, g2, beta2, residual, 
                 if s == 1:
                     broadcast_vectors()
                 if s == 2:
+                    keep_clock(h1raw[:, 0, 0, :], 1)
+                if s == 2:
+                    keep_clock(h1raw[:, 3, 0, :], 1)
+                if s == 2:
                     prepare_w2()
                 if s == 2:
                     h1_quantise(3)
                 if s == 3:
                     quantise_w2()
-                at(second_matmul, s - 4)
-                at(add_residual, s - 11)
-                at(store, s - 12)
                 at(add_bias, s - 4)
                 at(quantise_adj, s - 1)
                 at(quantise_agg, s - 3)
                 at(inverse_std, s - 6)
                 at(mean, s - 4)
                 at(centre_and_gain, s - 5)
-                at(transpose_adj, s - 0)
+                at(transpose0, s - 0)
+                at(transpose1, s - 0)
                 at(scale_and_shift, s - 7)
                 at(first_matmul, s - 2)
                 at(gelu, s - 9)
-                at(copy_adj, s - 0)
+                at(copy0, s - 0)
+                at(copy1, s - 0)
                 at(copy_agg, s - 2)
                 at(sum_squares, s - 4)
+                at(second_matmul, s - 3)
+                at(add_gpsimd, s - 10)
+                at(add_vector, s - 10)

@@ -17,7 +17,7 @@ FEAT = 512
 TILES = NODES // P
 PASSES = NODES // 512
 LN_EPS = 1e-5
-FIRST_ADD_ON_VECTOR = 12
+FIRST_ADD_ON_VECTOR = 10
 
 FLOPS = 2 * NODES * NODES * FEAT + 2 * NODES * FEAT * FEAT
 
@@ -28,7 +28,7 @@ def tile_multilayergnn_pb_kernel(tc, adj_norm, h1, W2, b2, g2, beta2, residual, 
         keep = ctx.enter_context(tc.tile_pool(name="keep", bufs=1))
         rot3 = ctx.enter_context(tc.tile_pool(name="rot3", bufs=4))
         rot4 = ctx.enter_context(tc.tile_pool(name="rot4", bufs=6))
-        rot6 = ctx.enter_context(tc.tile_pool(name="rot6", bufs=12))
+        rot6 = ctx.enter_context(tc.tile_pool(name="rot6", bufs=14))
         ps_tp = ctx.enter_context(tc.psum_pool(name="ps_tp", bufs=3))
         ps_agg = ctx.enter_context(tc.psum_pool(name="ps_agg", bufs=2))
         ps_lin = ctx.enter_context(tc.psum_pool(name="ps_lin", bufs=2))
@@ -83,10 +83,10 @@ def tile_multilayergnn_pb_kernel(tc, adj_norm, h1, W2, b2, g2, beta2, residual, 
         load_h1(1)
         load_h1(2)
         load_adj(0)
-        load_h1(3)
         load_vectors()
         load_adj(1)
         nc.sync.dma_start(out=w2raw[:], in_=W2.rearrange("(a p) h -> p a h", p=P))
+        load_h1(3)
         load_adj(2)
         load_adj(3)
         load_adj(4)
@@ -118,11 +118,6 @@ def tile_multilayergnn_pb_kernel(tc, adj_norm, h1, W2, b2, g2, beta2, residual, 
                 scales=h1s[:, g],
                 in_=h1g[:, g].rearrange("p h t -> p (h t)"),
             )
-
-        def keep_clock(source, count):
-            for _ in range(count):
-                scrap = ps_lin.tile([P, FEAT], F32, name="scrap", tag="lin")
-                nc.tensor.matmul(out=scrap[:], lhsT=identb[:], rhs=source, start=True, stop=True)
 
         def broadcast_vectors():
             pb = ps_lin.tile([P, FEAT], F32, tag="lin")
@@ -259,8 +254,8 @@ def tile_multilayergnn_pb_kernel(tc, adj_norm, h1, W2, b2, g2, beta2, residual, 
                 live[("ss2", i // 2)] = rot4.tile([P, 2], F32, name="ss", tag="ss")
             ss = live[("ss2", i // 2)][:, i % 2 : i % 2 + 1]
             nc.scalar.activation(
-                out=junk[:], in_=live[("y", i)][:], func=ACT.Square, bias=live[("mu", i)][:],
-                scale=-1.0, accum_out=ss,
+                out=junk[:], in_=live[("y", i)][:], func=ACT.Square, bias=live[("sumy", i)][:],
+                scale=-1.0 * FEAT, accum_out=ss,
             )
 
         def inverse_std(i):
@@ -271,7 +266,7 @@ def tile_multilayergnn_pb_kernel(tc, adj_norm, h1, W2, b2, g2, beta2, residual, 
             ve = rot4.tile([P, 2], F32, tag="ve")
             rstd = rot4.tile([P, 2], F32, tag="rstd")
             nc.gpsimd.tensor_scalar(
-                out=ve[:, cols], in0=live[("ss2", i // 2)][:, cols], scalar1=1.0 / FEAT, scalar2=LN_EPS,
+                out=ve[:, cols], in0=live[("ss2", i // 2)][:, cols], scalar1=1.0 / FEAT**3, scalar2=LN_EPS,
                 op0=ALU.mult, op1=ALU.add,
             )
             nc.gpsimd.tensor_tensor(out=rstd[:, cols], in0=ve[:, cols], in1=neghalf[:, cols], op=ALU.pow)
@@ -315,52 +310,44 @@ def tile_multilayergnn_pb_kernel(tc, adj_norm, h1, W2, b2, g2, beta2, residual, 
                 stage(i)
 
         with tc.manual_schedule():
-            for s in range(TILES + 10):
+            for s in range(TILES + 11):
                 if s == 0:
                     h1_regroup(0)
                 if s == 0:
                     h1_regroup(1)
                 if s == 0:
-                    h1_quantise(0)
-                if s == 0:
                     h1_regroup(2)
-                if s == 0:
-                    h1_quantise(1)
-                if s == 0:
-                    keep_clock(h1raw[:, 1, 0, :], 2)
-                if s == 0:
-                    keep_clock(h1raw[:, 2, 0, :], 2)
                 if s == 1:
-                    h1_regroup(3)
+                    h1_quantise(0)
+                if s == 1:
+                    h1_quantise(1)
                 if s == 1:
                     h1_quantise(2)
                 if s == 1:
                     broadcast_vectors()
                 if s == 2:
-                    keep_clock(h1raw[:, 0, 0, :], 1)
-                if s == 2:
-                    keep_clock(h1raw[:, 3, 0, :], 1)
-                if s == 2:
                     prepare_w2()
+                if s == 2:
+                    h1_regroup(3)
                 if s == 2:
                     h1_quantise(3)
                 if s == 3:
                     quantise_w2()
+                at(transpose0, s - 0)
+                at(gelu, s - 9)
                 at(add_bias, s - 4)
                 at(quantise_adj, s - 1)
                 at(quantise_agg, s - 3)
-                at(inverse_std, s - 6)
                 at(mean, s - 4)
-                at(centre_and_gain, s - 5)
-                at(transpose0, s - 0)
                 at(transpose1, s - 0)
-                at(scale_and_shift, s - 7)
-                at(first_matmul, s - 2)
-                at(gelu, s - 9)
+                at(add_vector, s - 11)
                 at(copy0, s - 0)
+                at(first_matmul, s - 2)
                 at(copy1, s - 0)
+                at(scale_and_shift, s - 7)
                 at(copy_agg, s - 2)
-                at(sum_squares, s - 4)
                 at(second_matmul, s - 3)
                 at(add_gpsimd, s - 10)
-                at(add_vector, s - 10)
+                at(sum_squares, s - 4)
+                at(centre_and_gain, s - 4)
+                at(inverse_std, s - 5)

@@ -82,8 +82,8 @@ def tile_multilayergnn_pb_kernel(tc, adj_norm, h1, W2, b2, g2, beta2, residual, 
         load_h1(0)
         load_h1(1)
         load_h1(2)
-        load_adj(0)
         load_vectors()
+        load_adj(0)
         load_adj(1)
         nc.sync.dma_start(out=w2raw[:], in_=W2.rearrange("(a p) h -> p a h", p=P))
         load_h1(3)
@@ -317,14 +317,14 @@ def tile_multilayergnn_pb_kernel(tc, adj_norm, h1, W2, b2, g2, beta2, residual, 
                     h1_regroup(1)
                 if s == 0:
                     h1_regroup(2)
+                if s == 0:
+                    broadcast_vectors()
                 if s == 1:
                     h1_quantise(0)
                 if s == 1:
                     h1_quantise(1)
                 if s == 1:
                     h1_quantise(2)
-                if s == 1:
-                    broadcast_vectors()
                 if s == 2:
                     prepare_w2()
                 if s == 2:
@@ -333,21 +333,21 @@ def tile_multilayergnn_pb_kernel(tc, adj_norm, h1, W2, b2, g2, beta2, residual, 
                     h1_quantise(3)
                 if s == 3:
                     quantise_w2()
-                at(transpose0, s - 0)
-                at(gelu, s - 9)
+                at(sum_squares, s - 5)
+                at(inverse_std, s - 6)
+                at(second_matmul, s - 4)
                 at(add_bias, s - 4)
-                at(quantise_adj, s - 1)
+                at(gelu, s - 9)
                 at(quantise_agg, s - 3)
-                at(mean, s - 4)
+                at(quantise_adj, s - 1)
+                at(transpose0, s - 0)
                 at(transpose1, s - 0)
+                at(centre_and_gain, s - 5)
+                at(mean, s - 4)
                 at(add_vector, s - 11)
                 at(copy0, s - 0)
                 at(first_matmul, s - 2)
-                at(copy1, s - 0)
                 at(scale_and_shift, s - 7)
+                at(copy1, s - 0)
                 at(copy_agg, s - 2)
-                at(second_matmul, s - 3)
                 at(add_gpsimd, s - 10)
-                at(sum_squares, s - 4)
-                at(centre_and_gain, s - 4)
-                at(inverse_std, s - 5)

from contextlib import ExitStack

import concourse.masks as masks
import concourse.mybir as mybir

FP8X4 = mybir.dt.float8_e4m3fn_x4
BF16 = mybir.dt.bfloat16
F32 = mybir.dt.float32
U32 = mybir.dt.uint32
U8 = mybir.dt.uint8
ALU = mybir.AluOpType
ACT = mybir.ActivationFunctionType

P = 128
NODES = 2048
FEAT = 512
TILES = NODES // P
PASSES = NODES // 512
LN_EPS = 1e-5
FIRST_ADD_ON_VECTOR = 10

FLOPS = 2 * NODES * NODES * FEAT + 2 * NODES * FEAT * FEAT


def tile_multilayergnn_pb_kernel(tc, adj_norm, h1, W2, b2, g2, beta2, residual, out):
    nc = tc.nc
    with ExitStack() as ctx:
        keep = ctx.enter_context(tc.tile_pool(name="keep", bufs=1))
        rot3 = ctx.enter_context(tc.tile_pool(name="rot3", bufs=4))
        rot4 = ctx.enter_context(tc.tile_pool(name="rot4", bufs=6))
        rot6 = ctx.enter_context(tc.tile_pool(name="rot6", bufs=14))
        ps_tp = ctx.enter_context(tc.psum_pool(name="ps_tp", bufs=3))
        ps_agg = ctx.enter_context(tc.psum_pool(name="ps_agg", bufs=2))
        ps_lin = ctx.enter_context(tc.psum_pool(name="ps_lin", bufs=2))
        ps_const = ctx.enter_context(tc.psum_pool(name="ps_const", bufs=1))

        adj_raw = [keep.tile([P, NODES], BF16, name="adj_raw%d" % i) for i in range(TILES)]
        res = [keep.tile([P, 4, FEAT], BF16, name="res%d" % c) for c in range(4)]
        h1raw = keep.tile([P, PASSES, 4, FEAT], BF16)
        h1g = keep.tile([P, PASSES, FEAT, 4], BF16, align_bytes=64)
        h1c = keep.tile([P, PASSES, FEAT], U32, align_bytes=64)
        h1s = keep.tile([P, PASSES, FEAT], U8, align_bytes=64)
        w2raw = keep.tile([P, 4, FEAT], BF16)
        w2g = keep.tile([P, 4, P, 4], BF16, align_bytes=64)
        w2c = keep.tile([P, FEAT], U32, align_bytes=64)
        w2s = keep.tile([P, FEAT], U8, align_bytes=64)
        vectors = keep.tile([P, 3, FEAT], BF16)
        ones = keep.tile([P, P], BF16)
        identf = keep.tile([P, P], F32)
        identb = keep.tile([P, P], BF16)
        neghalf = keep.tile([P, 2], F32)
        warm = keep.tile([P, 1], F32)
        b2bc = keep.tile([P, FEAT], F32)
        affine = ps_const.tile([P, 2, FEAT], BF16)
        gbc = affine[:, 0, :]
        betabc = affine[:, 1, :]

        nc.vector.memset(vectors[:], 0.0)
        nc.vector.memset(ones[:], 1.0)
        nc.vector.memset(neghalf[:], -0.5)
        masks.make_identity(nc, identf[:])
        masks.make_identity(nc, identb[:])

        adj_t = adj_norm.rearrange("(a p) k -> a p k", p=P)
        h1_t = h1.rearrange("(g u p e) h -> g p u (e h)", g=PASSES, u=2, p=P, e=2)
        res_t = residual.rearrange("(c a p) e -> c p a e", c=4, a=4, p=P)
        out_t = out.rearrange("(a p) e -> a p e", p=P)

        def load_adj(i):
            nc.sync.dma_start(out=adj_raw[i][:], in_=adj_t[i])

        def load_h1(g):
            nc.sync.dma_start(
                out=h1raw[:, g].rearrange("p (u e) h -> p u (e h)", u=2, e=2), in_=h1_t[g]
            )

        def load_vectors():
            for j, vec in enumerate((b2, g2, beta2)):
                nc.sync.dma_start(out=vectors[0:1, j, :], in_=vec.unsqueeze(0))

        nc.scalar.activation(out=warm[:], in_=neghalf[:, 0:1], func=ACT.Gelu)
        load_h1(0)
        load_h1(1)
        load_h1(2)
        load_vectors()
        load_adj(0)
        load_adj(1)
        nc.sync.dma_start(out=w2raw[:], in_=W2.rearrange("(a p) h -> p a h", p=P))
        load_h1(3)
        load_adj(2)
        load_adj(3)
        load_adj(4)
        nc.sync.dma_start(out=res[0][:], in_=res_t[0])
        load_adj(5)
        load_adj(6)
        load_adj(7)
        load_adj(8)
        nc.sync.dma_start(out=res[1][:], in_=res_t[1])
        load_adj(9)
        load_adj(10)
        load_adj(11)
        load_adj(12)
        nc.sync.dma_start(out=res[2][:], in_=res_t[2])
        load_adj(13)
        load_adj(14)
        load_adj(15)
        nc.sync.dma_start(out=res[3][:], in_=res_t[3])

        def h1_regroup(g):
            nc.vector.tensor_copy(
                out=h1g[:, g].rearrange("p (c i) t -> p c t i", i=4),
                in_=h1raw[:, g].rearrange("p t (c i) -> p c t i", i=4),
            )

        def h1_quantise(g):
            nc.vector.quantize_mx(
                out=h1c[:, g].bitcast(FP8X4),
                scales=h1s[:, g],
                in_=h1g[:, g].rearrange("p h t -> p (h t)"),
            )

        def broadcast_vectors():
            pb = ps_lin.tile([P, FEAT], F32, tag="lin")
            nc.tensor.matmul(out=pb[:], lhsT=ones[:], rhs=vectors[:, 0, :], start=True, stop=True)
            nc.scalar.copy(out=b2bc[:], in_=pb[:])
            nc.tensor.matmul(out=gbc, lhsT=ones[:], rhs=vectors[:, 1, :], start=True, stop=True)
            nc.tensor.matmul(out=betabc, lhsT=ones[:], rhs=vectors[:, 2, :], start=True, stop=True)

        def prepare_w2():
            for half in range(2):
                pw = ps_tp.tile([P, 2, 4, P], BF16, tag="tp")
                for a in range(2):
                    for t in range(4):
                        nc.tensor.transpose(
                            pw[:, a, t, :], w2raw[:, 2 * half + a, t * P : (t + 1) * P], identb[:]
                        )
                nc.scalar.copy(
                    out=w2g[:, 2 * half : 2 * half + 2], in_=pw[:].rearrange("p a t e -> p a e t")
                )

        def quantise_w2():
            nc.vector.quantize_mx(
                out=w2c[:].bitcast(FP8X4), scales=w2s[:], in_=w2g[:].rearrange("p a e t -> p (a e t)")
            )

        live = {}

        def transpose_half(i, b):
            words = adj_raw[i][:].bitcast(F32)
            tp = ps_tp.tile([P, 2, 2, P], F32, tag="tp")
            for gg in range(2):
                for u in range(2):
                    w0 = 256 * (2 * b + gg) + P * u
                    nc.tensor.transpose(tp[:, gg, u, :], words[:, w0 : w0 + P], identf[:])
            live[("tp", i, b)] = tp

        def copy_half(i, b):
            if b == 0:
                live[("adjg", i)] = rot3.tile([P, PASSES, P, 4], BF16, name="adjg", align_bytes=64, tag="adjg")
            adjgf = live[("adjg", i)][:].bitcast(F32)
            source = live[("tp", i, b)][:].rearrange("p g u i -> p g i u")
            if b == 1 and (False):
                nc.vector.tensor_copy(out=adjgf[:, 2 * b : 2 * b + 2], in_=source)
            else:
                nc.scalar.copy(out=adjgf[:, 2 * b : 2 * b + 2], in_=source)

        def transpose0(i):
            transpose_half(i, 0)

        def transpose1(i):
            transpose_half(i, 1)

        def copy0(i):
            copy_half(i, 0)

        def copy1(i):
            copy_half(i, 1)

        def quantise_adj(i):
            adjc = rot4.tile([P, PASSES * P], U32, align_bytes=64, tag="adjc")
            adjs = rot4.tile([P, PASSES * P], U8, align_bytes=64, tag="adjs")
            nc.vector.quantize_mx(
                out=adjc[:].bitcast(FP8X4),
                scales=adjs[:],
                in_=live[("adjg", i)][:].rearrange("p g i t -> p (g i t)"),
            )
            live[("adjq", i)] = (adjc, adjs)

        def first_matmul(i):
            adjc, adjs = live[("adjq", i)]
            aggp = ps_agg.tile([P, 4, P], F32, tag="agg")
            for t in range(4):
                for g in range(PASSES):
                    nc.tensor.matmul_mx(
                        out=aggp[:, t, :],
                        lhsT=h1c[:, g, t * P : (t + 1) * P].bitcast(FP8X4),
                        lhsT_scale=h1s[:, g, t * P : (t + 1) * P],
                        rhs=adjc[:, g * P : (g + 1) * P].bitcast(FP8X4),
                        rhs_scale=adjs[:, g * P : (g + 1) * P],
                        start=(g == 0),
                        stop=(g == PASSES - 1),
                    )
            live[("aggp", i)] = aggp

        def copy_agg(i):
            aggg = rot3.tile([P, P, 4], BF16, align_bytes=64, tag="aggg")
            nc.scalar.copy(out=aggg[:], in_=live[("aggp", i)][:].rearrange("p t i -> p i t"))
            live[("aggg", i)] = aggg

        def quantise_agg(i):
            aggc = rot3.tile([P, P], U32, align_bytes=64, tag="aggc")
            aggs = rot3.tile([P, P], U8, align_bytes=64, tag="aggs")
            nc.vector.quantize_mx(
                out=aggc[:].bitcast(FP8X4),
                scales=aggs[:],
                in_=live[("aggg", i)][:].rearrange("p i t -> p (i t)"),
            )
            live[("aggq", i)] = (aggc, aggs)

        def second_matmul(i):
            aggc, aggs = live[("aggq", i)]
            linp = ps_lin.tile([P, FEAT], F32, tag="lin")
            nc.tensor.matmul_mx(
                out=linp[:],
                lhsT=aggc[:].bitcast(FP8X4),
                lhsT_scale=aggs[:],
                rhs=w2c[:].bitcast(FP8X4),
                rhs_scale=w2s[:],
                start=True,
                stop=True,
            )
            live[("linp", i)] = linp

        def add_bias(i):
            y = rot4.tile([P, FEAT], F32, tag="y")
            sumy = rot4.tile([P, 1], F32, tag="sumy")
            nc.vector.scalar_tensor_tensor(
                out=y[:], in0=live[("linp", i)][:], scalar=1.0, in1=b2bc[:],
                op0=ALU.mult, op1=ALU.add, accum_out=sumy[:],
            )
            live[("y", i)] = y
            live[("sumy", i)] = sumy

        def mean(i):
            mu = rot4.tile([P, 1], F32, tag="mu")
            nc.vector.tensor_scalar(
                out=mu[:], in0=live[("sumy", i)][:], scalar1=1.0 / FEAT, scalar2=None, op0=ALU.mult
            )
            live[("mu", i)] = mu

        def sum_squares(i):
            junk = rot3.tile([P, FEAT], F32, tag="junk")
            if i % 2 == 0:
                live[("ss2", i // 2)] = rot4.tile([P, 2], F32, name="ss", tag="ss")
            ss = live[("ss2", i // 2)][:, i % 2 : i % 2 + 1]
            nc.scalar.activation(
                out=junk[:], in_=live[("y", i)][:], func=ACT.Square, bias=live[("sumy", i)][:],
                scale=-1.0 * FEAT, accum_out=ss,
            )

        def inverse_std(i):
            first = i if i >= TILES - 2 else i - 1
            if first % 2 == 1 and i < TILES - 2 or first < 0:
                return
            cols = slice(first % 2, i % 2 + 1)
            ve = rot4.tile([P, 2], F32, tag="ve")
            rstd = rot4.tile([P, 2], F32, tag="rstd")
            nc.gpsimd.tensor_scalar(
                out=ve[:, cols], in0=live[("ss2", i // 2)][:, cols], scalar1=1.0 / FEAT**3, scalar2=LN_EPS,
                op0=ALU.mult, op1=ALU.add,
            )
            nc.gpsimd.tensor_tensor(out=rstd[:, cols], in0=ve[:, cols], in1=neghalf[:, cols], op=ALU.pow)
            for j in range(first, i + 1):
                live[("rstd", j)] = rstd[:, j % 2 : j % 2 + 1]

        def centre_and_gain(i):
            t = rot6.tile([P, FEAT], F32, tag="t")
            nc.vector.scalar_tensor_tensor(
                out=t[:], in0=live[("y", i)][:], scalar=live[("mu", i)][:], in1=gbc,
                op0=ALU.subtract, op1=ALU.mult,
            )
            live[("t", i)] = t

        def scale_and_shift(i):
            t = live[("t", i)]
            nc.vector.scalar_tensor_tensor(
                out=t[:], in0=t[:], scalar=live[("rstd", i)], in1=betabc,
                op0=ALU.mult, op1=ALU.add,
            )

        def gelu(i):
            t = live[("t", i)]
            nc.scalar.activation(out=t[:], in_=t[:], func=ACT.Gelu)

        def add_residual(engine, i):
            t = live[("t", i)][:]
            engine.tensor_tensor(out=t, in0=t, in1=res[i // 4][:, i % 4, :], op=ALU.add)
            nc.sync.dma_start(out=out_t[i], in_=t)

        def add_gpsimd(i):
            if i < FIRST_ADD_ON_VECTOR:
                add_residual(nc.gpsimd, i)

        def add_vector(i):
            if i >= FIRST_ADD_ON_VECTOR:
                add_residual(nc.vector, i)

        def at(stage, i):
            if 0 <= i < TILES:
                stage(i)

        with tc.manual_schedule():
            for s in range(TILES + 11):
                if s == 0:
                    h1_regroup(0)
                if s == 0:
                    h1_regroup(1)
                if s == 0:
                    h1_regroup(2)
                if s == 0:
                    broadcast_vectors()
                if s == 1:
                    h1_quantise(0)
                if s == 1:
                    h1_quantise(1)
                if s == 1:
                    h1_quantise(2)
                if s == 2:
                    prepare_w2()
                if s == 2:
                    h1_regroup(3)
                if s == 2:
                    h1_quantise(3)
                if s == 3:
                    quantise_w2()
                at(sum_squares, s - 5)
                at(inverse_std, s - 6)
                at(second_matmul, s - 4)
                at(add_bias, s - 4)
                at(gelu, s - 9)
                at(quantise_agg, s - 3)
                at(quantise_adj, s - 1)
                at(transpose0, s - 0)
                at(transpose1, s - 0)
                at(centre_and_gain, s - 5)
                at(mean, s - 4)
                at(add_vector, s - 11)
                at(copy0, s - 0)
                at(first_matmul, s - 2)
                at(scale_and_shift, s - 7)
                at(copy1, s - 0)
                at(copy_agg, s - 2)
                at(add_gpsimd, s - 10)
